import numpy as np
import ml_dtypes


def mxq(x, axis, fmt="e4m3"):
    dtype, down = {"e4m3": (ml_dtypes.float8_e4m3fn, 7), "e5m2": (ml_dtypes.float8_e5m2, 14)}[fmt]
    v = np.moveaxis(np.asarray(x, np.float32).astype(ml_dtypes.bfloat16).astype(np.float64), axis, -1)
    blocks = v.reshape(v.shape[:-1] + (-1, 32))
    amax = np.abs(blocks).max(-1, keepdims=True)
    byte = np.maximum(np.where(amax > 0, np.frexp(amax)[1] - 1 + 127, 0) - down, 1)
    scale = np.exp2(byte - 127.0)
    codes = (blocks / scale).astype(np.float32).astype(dtype).astype(np.float64)
    return np.moveaxis((codes * scale).reshape(v.shape), -1, axis)


WIDE = False


def mx_kscale(k):
    if not WIDE:
        return np.ones(k)
    levels = np.array([10, -10, 5, -5, 0])
    a = np.random.permutation(np.resize(levels, k // 512 * 4)).reshape(k // 512, 4)
    idx = np.arange(k)
    return np.exp2(a[idx // 512, idx % 128 // 32])


BF16 = ml_dtypes.bfloat16


def bf(x):
    return np.asarray(x, np.float32).astype(BF16)


def f64(x):
    return np.asarray(x).astype(np.float64)


N, T, C, D, H, DO = 4, 256, 1024, 1024, 16, 1024
HD = D // H


def head_scores(q, k):
    return np.stack([(q * k[:, :, g:g + 1, :]).sum(-1) for g in range(H)], axis=-1)


def setup_inputs():
    s = mx_kscale(C)
    return {"x": bf(np.random.standard_normal((N, T, C)) * s),
            "w_qk": bf(np.random.standard_normal((C, 2 * D)) / np.sqrt(C) / s[:, None]),
            "b_qk": bf(np.random.standard_normal(2 * D) * 0.3)}


def reference(x, w_qk, b_qk):
    qk = (mxq(f64(x), 2, "e4m3") @ mxq(f64(w_qk), 0, "e4m3")) + f64(b_qk)
    qk = qk.reshape(N, T, 2, H, HD)
    q, k = qk[:, :, 0], qk[:, :, 1]
    s = head_scores(q * HD ** -0.5, k)
    e = np.exp(s - s.max(-1, keepdims=True))
    return e / e.sum(-1, keepdims=True)

@@ -1,0 +1,255 @@
+from contextlib import ExitStack
+
+import concourse.mybir as mybir
+from concourse.masks import make_identity
+
+F32 = mybir.dt.float32
+BF16 = mybir.dt.bfloat16
+I32 = mybir.dt.int32
+U32 = mybir.dt.uint32
+U8 = mybir.dt.uint8
+FP8X4 = mybir.dt.float8_e4m3fn_x4
+ALU = mybir.AluOpType
+ACT = mybir.ActivationFunctionType
+AXIS = mybir.AxisListType
+
+P = 128
+TOKENS = 1024
+C = 1024
+HEADS = 16
+HD = 64
+K_PASS = 512
+PASSES = C // K_PASS
+PAIRS = TOKENS // 2
+GROUP = 4
+CHUNK = 128
+CHUNKS = PAIRS // CHUNK
+CHUNK_GROUPS = CHUNK // GROUP
+BANK_GROUPS = 8
+BANK_HEADS = 4
+W_BLOCK = 512
+SLOT = 2 * HD
+
+FLOPS = 2 * TOKENS * C * 2 * HEADS * HD + 2 * TOKENS * HEADS * HEADS * HD
+
+
+def tile_attention_pa_kernel(tc, x, w_qk, b_qk, out):
+    nc = tc.nc
+    x_rows = x.rearrange("n t c -> (n t) c")
+    out_rows = out.rearrange("n t h g -> (n t h) g").rearrange("(G p) g -> p G g", p=P)
+
+    with ExitStack() as ctx:
+        keep = ctx.enter_context(tc.tile_pool(name="keep", bufs=1))
+        x_in = ctx.enter_context(tc.tile_pool(name="x_in", bufs=CHUNKS))
+        w_in = ctx.enter_context(tc.tile_pool(name="w_in", bufs=4))
+        w_stage = ctx.enter_context(tc.tile_pool(name="w_stage", bufs=3))
+        q_pool = ctx.enter_context(tc.tile_pool(name="q_pool", bufs=2))
+        soft = ctx.enter_context(tc.tile_pool(name="soft", bufs=2))
+        psum = ctx.enter_context(tc.psum_pool(name="psum", bufs=4))
+
+        x_grouped = keep.tile([P, PASSES, 2, PAIRS, 4], BF16, align_bytes=64)
+        x_codes = keep.tile([P, PASSES, 2, PAIRS], U32, align_bytes=64)
+        x_scales = keep.tile([P, PASSES, 2, PAIRS], U8, align_bytes=64)
+        w_cols = (2 * HEADS + 1) * SLOT
+        w_codes = keep.tile([P, PASSES, w_cols], U32, align_bytes=64)
+        w_scales = keep.tile([P, PASSES, w_cols], U8, align_bytes=64)
+        k_t = keep.tile([P, PAIRS // GROUP, HEADS, GROUP], F32)
+
+        nc.vector.memset(
+            w_codes[:].bitcast(I32).rearrange("p c (s b f) -> p c s b f", b=2, f=HD)[:, :, :, 0, :], 0
+        )
+        nc.vector.memset(
+            w_scales[:].bitcast(I32).rearrange("p c (s b f) -> p c s b f", b=2, f=HD // 4)[:, :, :, 0, :], 0
+        )
+
+        identity = keep.tile([P, P], F32)
+        make_identity(nc, identity[:])
+
+        def load_w_block(block):
+            cols = slice(block * W_BLOCK, (block + 1) * W_BLOCK)
+            w_raw = w_in.tile([P, PASSES, 4, W_BLOCK], BF16, name="w_raw")
+            for c in range(PASSES):
+                for u in range(2):
+                    first = K_PASS * c + 256 * u
+                    nc.sync.dma_start(
+                        out=w_raw[:, c, 2 * u : 2 * u + 2, :],
+                        in_=w_qk[first : first + 256, cols].rearrange("(p e) f -> p e f", e=2),
+                    )
+            return w_raw
+
+        def load_x_chunk(ch):
+            x_raw = x_in.tile([P, 2, C], BF16, name="x_raw")
+            rows = x_rows[2 * CHUNK * ch : 2 * CHUNK * (ch + 1), :]
+            nc.sync.dma_start(out=x_raw[:], in_=rows.rearrange("(r p) c -> p r c", p=P))
+            return x_raw
+
+        w_raws = {}
+        w_raws[2] = load_w_block(2)
+        x_raws = [load_x_chunk(ch) for ch in range(CHUNKS)]
+        w_raws[3] = load_w_block(3)
+        w_raws[0] = load_w_block(0)
+        w_raws[1] = load_w_block(1)
+
+        bias_rows = keep.tile([P, P], BF16)
+        nc.vector.memset(bias_rows[:], 0.0)
+        for a in range(2):
+            nc.scalar.dma_start(
+                out=bias_rows[0 : 2 * HEADS, HD * a : HD * (a + 1)],
+                in_=b_qk.rearrange("(f d) -> f d", d=HD),
+            )
+        bias_rows_f32 = keep.tile([P, P], F32)
+        nc.vector.tensor_copy(out=bias_rows_f32[:], in_=bias_rows[:])
+        bias_t = psum.tile([P, P], F32, tag="acc")
+        nc.tensor.transpose(bias_t[:], bias_rows_f32[:], identity[:])
+        k_bias = keep.tile([P, HEADS], F32)
+        nc.vector.tensor_copy(out=k_bias[:], in_=bias_t[:, HEADS : 2 * HEADS])
+        q_bias = keep.tile([P, 2, HEADS], F32)
+        nc.vector.memset(q_bias[:], 0.0)
+        for a in range(2):
+            half = slice(HD * a, HD * (a + 1))
+            nc.vector.tensor_scalar_mul(out=q_bias[half, a, :], in0=bias_t[half, 0:HEADS], scalar1=0.125)
+
+        def quantise_w_block(block):
+            for c in range(PASSES):
+                w_grouped = w_stage.tile([P, W_BLOCK, 4], BF16, name="w_grouped", align_bytes=64)
+                nc.vector.tensor_copy(
+                    out=w_grouped[:].rearrange("p (f i) t -> p f t i", i=4),
+                    in_=w_raws[block][:, c].rearrange("p t (f i) -> p f t i", i=4),
+                )
+                for j in range(W_BLOCK // HD):
+                    head = block * (W_BLOCK // HD) + j
+                    cols = slice(SLOT * head + HD, SLOT * (head + 1))
+                    nc.vector.quantize_mx(
+                        out=w_codes[:, c, cols].bitcast(FP8X4),
+                        scales=w_scales[:, c, cols],
+                        in_=w_grouped[:, HD * j : HD * (j + 1), :].rearrange("p f t -> p (f t)"),
+                    )
+
+        x_grouped_words = x_grouped[:].bitcast(F32)
+
+        def quantise_x_chunk(ch):
+            for r in range(2):
+                words = x_raws[ch][:, r, :].bitcast(F32)
+                x_t = psum.tile([P, PASSES, 2, P], F32, tag="acc")
+                for c in range(PASSES):
+                    for u in range(2):
+                        first = 256 * c + P * u
+                        nc.tensor.transpose(x_t[:, c, u, :], words[:, first : first + P], identity[:])
+                pairs = slice(CHUNK * ch + 64 * r, CHUNK * ch + 64 * (r + 1))
+                for c in range(PASSES):
+                    nc.scalar.copy(
+                        out=x_grouped_words[:, c, :, pairs, :],
+                        in_=x_t[:, c].rearrange("p u (m a) -> p a m u", a=2),
+                    )
+            pairs = slice(CHUNK * ch, CHUNK * (ch + 1))
+            for c in range(PASSES):
+                for a in range(2):
+                    nc.vector.quantize_mx(
+                        out=x_codes[:, c, a, pairs].bitcast(FP8X4),
+                        scales=x_scales[:, c, a, pairs],
+                        in_=x_grouped[:, c, a, pairs, :].rearrange("p n t -> p (n t)"),
+                    )
+
+        quantise_w_block(2)
+        for ch in range(CHUNKS):
+            quantise_x_chunk(ch)
+        quantise_w_block(3)
+        quantise_w_block(0)
+        quantise_w_block(1)
+
+        def project(acc, head, a, pairs, start, stop):
+            window = slice(SLOT * head + HD * (1 - a), SLOT * head + HD * (1 - a) + P)
+            for c in range(PASSES):
+                nc.tensor.matmul_mx(
+                    out=acc,
+                    lhsT=w_codes[:, c, window].bitcast(FP8X4),
+                    lhsT_scale=w_scales[:, c, window],
+                    rhs=x_codes[:, c, a, pairs].bitcast(FP8X4),
+                    rhs_scale=x_scales[:, c, a, pairs],
+                    start=start and c == 0,
+                    stop=stop and c == PASSES - 1,
+                )
+
+        for g in range(HEADS):
+            k_acc = psum.tile([P, PAIRS], F32, tag="acc")
+            project(k_acc[:], HEADS + g, 0, slice(0, PAIRS), True, False)
+            project(k_acc[:], HEADS + g, 1, slice(0, PAIRS), False, True)
+            nc.scalar.activation(
+                out=k_t[:, :, g, :],
+                in_=k_acc[:].rearrange("p (G u) -> p G u", u=GROUP),
+                func=ACT.Identity,
+                bias=k_bias[:, g : g + 1],
+                scale=1.0,
+            )
+
+        def project_q_bank(ch, bank, q_s):
+            a, first_head = bank // (HEADS // BANK_HEADS), BANK_HEADS * (bank % (HEADS // BANK_HEADS))
+            q_acc = psum.tile([P, BANK_HEADS, CHUNK], F32, tag="acc")
+            for j in range(BANK_HEADS):
+                project(q_acc[:, j, :], first_head + j, a, slice(CHUNK * ch, CHUNK * (ch + 1)), True, True)
+            heads = slice(first_head, first_head + BANK_HEADS)
+            nc.vector.scalar_tensor_tensor(
+                out=q_s[:, :, a, heads],
+                in0=q_acc[:].rearrange("p h n -> p n h"),
+                scalar=0.125,
+                in1=q_bias[:, a, heads].unsqueeze(1).to_broadcast([P, CHUNK, BANK_HEADS]),
+                op0=ALU.mult,
+                op1=ALU.add,
+            )
+
+        def score_groups(ch, first, count, q_s, score_acc, scores):
+            for i in range(first, first + count):
+                nc.tensor.matmul(
+                    out=score_acc[:, i % BANK_GROUPS],
+                    lhsT=q_s[:, GROUP * i : GROUP * (i + 1)].rearrange("p u a h -> p (u a h)"),
+                    rhs=k_t[:, CHUNK_GROUPS * ch + i].rearrange("p g u -> p (g u)"),
+                    start=True,
+                    stop=True,
+                )
+            if (first + count) % BANK_GROUPS == 0:
+                groups = slice(first + count - BANK_GROUPS, first + count)
+                for u in range(GROUP):
+                    quadrant = slice(32 * u, 32 * (u + 1))
+                    nc.scalar.copy(
+                        out=scores[quadrant, groups, :],
+                        in_=score_acc[quadrant].rearrange("p G (g u) -> p G g u", u=GROUP)[:, :, :, u],
+                    )
+
+        def softmax_and_store(ch, scores):
+            shape = [P, CHUNK_GROUPS, HEADS]
+            top = soft.tile([P, CHUNK_GROUPS], F32, name="top")
+            nc.vector.tensor_reduce(out=top[:], in_=scores[:], axis=AXIS.X, op=ALU.max)
+            shifted = soft.tile(shape, F32, name="shifted")
+            nc.vector.tensor_tensor(
+                out=shifted[:], in0=scores[:], in1=top[:].unsqueeze(2).to_broadcast(shape), op=ALU.subtract
+            )
+            weights = soft.tile(shape, F32, name="weights")
+            nc.scalar.activation(out=weights[:], in_=shifted[:], func=ACT.Exp)
+            total = soft.tile([P, CHUNK_GROUPS], F32, name="total")
+            nc.vector.tensor_reduce(out=total[:], in_=weights[:], axis=AXIS.X, op=ALU.add)
+            inverse = soft.tile([P, CHUNK_GROUPS], F32, name="inverse")
+            nc.vector.reciprocal(out=inverse[:], in_=total[:])
+            result = soft.tile(shape, F32, name="result")
+            nc.vector.tensor_tensor(
+                out=result[:], in0=weights[:], in1=inverse[:].unsqueeze(2).to_broadcast(shape), op=ALU.mult
+            )
+            nc.sync.dma_start(out=out_rows[:, CHUNK_GROUPS * ch : CHUNK_GROUPS * (ch + 1), :], in_=result[:])
+
+        q_banks = 2 * HEADS // BANK_HEADS
+        groups_per_bank = CHUNK_GROUPS // q_banks
+        q_tiles = {}
+        for ch in range(CHUNKS + 1):
+            if ch < CHUNKS:
+                q_tiles[ch] = q_pool.tile([P, CHUNK, 2, HEADS], F32, name="q_s")
+            if ch > 0:
+                scores = soft.tile([P, CHUNK_GROUPS, HEADS], F32, name="scores")
+            for bank in range(q_banks):
+                if ch < CHUNKS:
+                    project_q_bank(ch, bank, q_tiles[ch])
+                if ch > 0:
+                    first = groups_per_bank * bank
+                    if first % BANK_GROUPS == 0:
+                        score_acc = psum.tile([P, BANK_GROUPS, HEADS * GROUP], F32, name="score_acc")
+                    score_groups(ch - 1, first, groups_per_bank, q_tiles[ch - 1], score_acc, scores)
+            if ch > 0:
+                softmax_and_store(ch - 1, scores)

@@ -5,7 +5,6 @@ from concourse.masks import make_identity
 
 F32 = mybir.dt.float32
 BF16 = mybir.dt.bfloat16
-I32 = mybir.dt.int32
 U32 = mybir.dt.uint32
 U8 = mybir.dt.uint8
 FP8X4 = mybir.dt.float8_e4m3fn_x4
@@ -21,14 +20,15 @@ HD = 64
 K_PASS = 512
 PASSES = C // K_PASS
 PAIRS = TOKENS // 2
-GROUP = 4
 CHUNK = 128
 CHUNKS = PAIRS // CHUNK
-CHUNK_GROUPS = CHUNK // GROUP
+W_BLOCK = 512
+BLOCK_HEADS = W_BLOCK // HD
+GROUP = 4
 BANK_GROUPS = 8
 BANK_HEADS = 4
-W_BLOCK = 512
-SLOT = 2 * HD
+Q_BANKS = HEADS // BANK_HEADS
+LAG = Q_BANKS
 
 FLOPS = 2 * TOKENS * C * 2 * HEADS * HD + 2 * TOKENS * HEADS * HEADS * HD
 
@@ -39,185 +39,199 @@ def tile_attention_pa_kernel(tc, x, w_qk, b_qk, out):
     out_rows = out.rearrange("n t h g -> (n t h) g").rearrange("(G p) g -> p G g", p=P)
 
     with ExitStack() as ctx:
+        ctx.enter_context(tc.manual_schedule())
         keep = ctx.enter_context(tc.tile_pool(name="keep", bufs=1))
-        x_in = ctx.enter_context(tc.tile_pool(name="x_in", bufs=CHUNKS))
-        w_in = ctx.enter_context(tc.tile_pool(name="w_in", bufs=4))
-        w_stage = ctx.enter_context(tc.tile_pool(name="w_stage", bufs=3))
-        q_pool = ctx.enter_context(tc.tile_pool(name="q_pool", bufs=2))
-        soft = ctx.enter_context(tc.tile_pool(name="soft", bufs=2))
         psum = ctx.enter_context(tc.psum_pool(name="psum", bufs=4))
 
-        x_grouped = keep.tile([P, PASSES, 2, PAIRS, 4], BF16, align_bytes=64)
-        x_codes = keep.tile([P, PASSES, 2, PAIRS], U32, align_bytes=64)
-        x_scales = keep.tile([P, PASSES, 2, PAIRS], U8, align_bytes=64)
-        w_cols = (2 * HEADS + 1) * SLOT
-        w_codes = keep.tile([P, PASSES, w_cols], U32, align_bytes=64)
-        w_scales = keep.tile([P, PASSES, w_cols], U8, align_bytes=64)
+        x_codes = keep.tile([P, CHUNKS, PASSES, 2, CHUNK], U32, align_bytes=64)
+        x_scales = keep.tile([P, CHUNKS, PASSES, 2, CHUNK], U8, align_bytes=64)
+        w_codes = keep.tile([P, PASSES, 2 * HEADS * HD], U32, align_bytes=64)
+        w_scales = keep.tile([P, PASSES, 2 * HEADS * HD], U8, align_bytes=64)
+        qk_rows = [keep.tile([P, 2 * HEADS, 2, HD], F32, name="qk_rows%d" % ch) for ch in range(CHUNKS)]
         k_t = keep.tile([P, PAIRS // GROUP, HEADS, GROUP], F32)
-
-        nc.vector.memset(
-            w_codes[:].bitcast(I32).rearrange("p c (s b f) -> p c s b f", b=2, f=HD)[:, :, :, 0, :], 0
-        )
-        nc.vector.memset(
-            w_scales[:].bitcast(I32).rearrange("p c (s b f) -> p c s b f", b=2, f=HD // 4)[:, :, :, 0, :], 0
-        )
-
-        identity = keep.tile([P, P], F32)
-        make_identity(nc, identity[:])
-
-        def load_w_block(block):
-            cols = slice(block * W_BLOCK, (block + 1) * W_BLOCK)
-            w_raw = w_in.tile([P, PASSES, 4, W_BLOCK], BF16, name="w_raw")
-            for c in range(PASSES):
-                for u in range(2):
-                    first = K_PASS * c + 256 * u
-                    nc.sync.dma_start(
-                        out=w_raw[:, c, 2 * u : 2 * u + 2, :],
-                        in_=w_qk[first : first + 256, cols].rearrange("(p e) f -> p e f", e=2),
-                    )
-            return w_raw
-
-        def load_x_chunk(ch):
-            x_raw = x_in.tile([P, 2, C], BF16, name="x_raw")
-            rows = x_rows[2 * CHUNK * ch : 2 * CHUNK * (ch + 1), :]
-            nc.sync.dma_start(out=x_raw[:], in_=rows.rearrange("(r p) c -> p r c", p=P))
-            return x_raw
-
-        w_raws = {}
-        w_raws[2] = load_w_block(2)
-        x_raws = [load_x_chunk(ch) for ch in range(CHUNKS)]
-        w_raws[3] = load_w_block(3)
-        w_raws[0] = load_w_block(0)
-        w_raws[1] = load_w_block(1)
-
         bias_rows = keep.tile([P, P], BF16)
+        bias_rows_f32 = keep.tile([P, P], F32)
+        k_bias = keep.tile([P, HEADS], F32)
+        q_bias = keep.tile([P, 2, HEADS], F32)
+        q_scale = keep.tile([P, 2], F32)
+        identity = keep.tile([P, P], F32)
+
         nc.vector.memset(bias_rows[:], 0.0)
         for a in range(2):
             nc.scalar.dma_start(
                 out=bias_rows[0 : 2 * HEADS, HD * a : HD * (a + 1)],
                 in_=b_qk.rearrange("(f d) -> f d", d=HD),
             )
-        bias_rows_f32 = keep.tile([P, P], F32)
+        make_identity(nc, identity[:])
+        nc.vector.memset(q_bias[:], 0.0)
+        nc.vector.memset(q_scale[:], 0.0)
         nc.vector.tensor_copy(out=bias_rows_f32[:], in_=bias_rows[:])
         bias_t = psum.tile([P, P], F32, tag="acc")
         nc.tensor.transpose(bias_t[:], bias_rows_f32[:], identity[:])
-        k_bias = keep.tile([P, HEADS], F32)
         nc.vector.tensor_copy(out=k_bias[:], in_=bias_t[:, HEADS : 2 * HEADS])
-        q_bias = keep.tile([P, 2, HEADS], F32)
-        nc.vector.memset(q_bias[:], 0.0)
         for a in range(2):
             half = slice(HD * a, HD * (a + 1))
+            nc.vector.memset(q_scale[half, a : a + 1], 0.125)
             nc.vector.tensor_scalar_mul(out=q_bias[half, a, :], in0=bias_t[half, 0:HEADS], scalar1=0.125)
 
-        def quantise_w_block(block):
-            for c in range(PASSES):
-                w_grouped = w_stage.tile([P, W_BLOCK, 4], BF16, name="w_grouped", align_bytes=64)
-                nc.vector.tensor_copy(
-                    out=w_grouped[:].rearrange("p (f i) t -> p f t i", i=4),
-                    in_=w_raws[block][:, c].rearrange("p t (f i) -> p f t i", i=4),
+        with tc.tile_pool(name="stage", bufs=4) as stage:
+
+            def load_x_chunk(ch):
+                x_raw = stage.tile([P, 2, C], BF16, name="x_raw")
+                rows = x_rows[2 * CHUNK * ch : 2 * CHUNK * (ch + 1), :]
+                nc.sync.dma_start(out=x_raw[:], in_=rows.rearrange("(r p) c -> p r c", p=P))
+                return x_raw
+
+            def load_w_block(block):
+                cols = slice(block * W_BLOCK, (block + 1) * W_BLOCK)
+                w_raw = stage.tile([P, PASSES, 4, W_BLOCK], BF16, name="w_raw")
+                for c in range(PASSES):
+                    for u in range(2):
+                        first = K_PASS * c + 256 * u
+                        nc.sync.dma_start(
+                            out=w_raw[:, c, 2 * u : 2 * u + 2, :],
+                            in_=w_qk[first : first + 256, cols].rearrange("(p e) f -> p e f", e=2),
+                        )
+                return w_raw
+
+            def transpose_x_chunk(x_raw):
+                x_grouped = stage.tile([P, PASSES, 2, CHUNK, 4], BF16, name="x_grouped", align_bytes=64)
+                x_grouped_words = x_grouped[:].bitcast(F32)
+                for r in range(2):
+                    words = x_raw[:, r, :].bitcast(F32)
+                    x_t = psum.tile([P, PASSES, 2, P], F32, tag="acc")
+                    for c in range(PASSES):
+                        for u in range(2):
+                            first = 256 * c + P * u
+                            nc.tensor.transpose(x_t[:, c, u, :], words[:, first : first + P], identity[:])
+                    for c in range(PASSES):
+                        nc.scalar.copy(
+                            out=x_grouped_words[:, c, :, 64 * r : 64 * (r + 1), :],
+                            in_=x_t[:, c].rearrange("p u (m a) -> p a m u", a=2),
+                        )
+                return x_grouped
+
+            def quantise_x_chunk(ch, x_grouped):
+                nc.vector.quantize_mx(
+                    out=x_codes[:, ch].rearrange("p c a n -> p (c a n)").bitcast(FP8X4),
+                    scales=x_scales[:, ch].rearrange("p c a n -> p (c a n)"),
+                    in_=x_grouped[:].rearrange("p c a n t -> p (c a n t)"),
                 )
-                for j in range(W_BLOCK // HD):
-                    head = block * (W_BLOCK // HD) + j
-                    cols = slice(SLOT * head + HD, SLOT * (head + 1))
+
+            def quantise_w_block(block, w_raw):
+                cols = slice(block * W_BLOCK, (block + 1) * W_BLOCK)
+                grouped = []
+                for c in range(PASSES):
+                    w_grouped = stage.tile([P, W_BLOCK, 4], BF16, name="w_grouped", align_bytes=64)
+                    nc.vector.tensor_copy(
+                        out=w_grouped[:].rearrange("p (f i) t -> p f t i", i=4),
+                        in_=w_raw[:, c].rearrange("p t (f i) -> p f t i", i=4),
+                    )
+                    grouped.append(w_grouped)
+                for c in range(PASSES):
                     nc.vector.quantize_mx(
                         out=w_codes[:, c, cols].bitcast(FP8X4),
                         scales=w_scales[:, c, cols],
-                        in_=w_grouped[:, HD * j : HD * (j + 1), :].rearrange("p f t -> p (f t)"),
+                        in_=grouped[c][:].rearrange("p f t -> p (f t)"),
                     )
 
-        x_grouped_words = x_grouped[:].bitcast(F32)
+            def project_block(block):
+                cols = slice(block * W_BLOCK, (block + 1) * W_BLOCK)
+                heads = slice(block * BLOCK_HEADS, (block + 1) * BLOCK_HEADS)
+                for ch in range(CHUNKS):
+                    for a in range(2):
+                        acc = psum.tile([P, BLOCK_HEADS, HD], F32, tag="acc")
+                        for c in range(PASSES):
+                            nc.tensor.matmul_mx(
+                                out=acc[:].rearrange("p h d -> p (h d)"),
+                                lhsT=x_codes[:, ch, c, a, :].bitcast(FP8X4),
+                                lhsT_scale=x_scales[:, ch, c, a, :],
+                                rhs=w_codes[:, c, cols].bitcast(FP8X4),
+                                rhs_scale=w_scales[:, c, cols],
+                                start=(c == 0),
+                                stop=(c == PASSES - 1),
+                            )
+                        copy_out = nc.vector.tensor_copy if ch == CHUNKS - 1 else nc.scalar.copy
+                        copy_out(out=qk_rows[ch][:, heads, a, :], in_=acc[:])
 
-        def quantise_x_chunk(ch):
-            for r in range(2):
-                words = x_raws[ch][:, r, :].bitcast(F32)
-                x_t = psum.tile([P, PASSES, 2, P], F32, tag="acc")
-                for c in range(PASSES):
-                    for u in range(2):
-                        first = 256 * c + P * u
-                        nc.tensor.transpose(x_t[:, c, u, :], words[:, first : first + P], identity[:])
-                pairs = slice(CHUNK * ch + 64 * r, CHUNK * ch + 64 * (r + 1))
-                for c in range(PASSES):
-                    nc.scalar.copy(
-                        out=x_grouped_words[:, c, :, pairs, :],
-                        in_=x_t[:, c].rearrange("p u (m a) -> p a m u", a=2),
-                    )
-            pairs = slice(CHUNK * ch, CHUNK * (ch + 1))
-            for c in range(PASSES):
-                for a in range(2):
-                    nc.vector.quantize_mx(
-                        out=x_codes[:, c, a, pairs].bitcast(FP8X4),
-                        scales=x_scales[:, c, a, pairs],
-                        in_=x_grouped[:, c, a, pairs, :].rearrange("p n t -> p (n t)"),
-                    )
+            blocks = (2, 3, 0, 1)
+            x_raws = [load_x_chunk(0)]
+            w_raws = {blocks[0]: load_w_block(blocks[0])}
+            x_raws.extend([load_x_chunk(ch) for ch in range(1, CHUNKS)])
+            for block in blocks[1:]:
+                w_raws[block] = load_w_block(block)
 
-        quantise_w_block(2)
-        for ch in range(CHUNKS):
-            quantise_x_chunk(ch)
-        quantise_w_block(3)
-        quantise_w_block(0)
-        quantise_w_block(1)
+            x_groupeds = [transpose_x_chunk(x_raws[0])]
+            quantise_x_chunk(0, x_groupeds[0])
+            x_groupeds.extend([transpose_x_chunk(x_raws[ch]) for ch in range(1, CHUNKS)])
+            quantise_w_block(blocks[0], w_raws[blocks[0]])
+            for ch in range(1, CHUNKS):
+                quantise_x_chunk(ch, x_groupeds[ch])
+            for i in range(len(blocks)):
+                if i + 1 < len(blocks):
+                    quantise_w_block(blocks[i + 1], w_raws[blocks[i + 1]])
+                project_block(blocks[i])
 
-        def project(acc, head, a, pairs, start, stop):
-            window = slice(SLOT * head + HD * (1 - a), SLOT * head + HD * (1 - a) + P)
-            for c in range(PASSES):
-                nc.tensor.matmul_mx(
-                    out=acc,
-                    lhsT=w_codes[:, c, window].bitcast(FP8X4),
-                    lhsT_scale=w_scales[:, c, window],
-                    rhs=x_codes[:, c, a, pairs].bitcast(FP8X4),
-                    rhs_scale=x_scales[:, c, a, pairs],
-                    start=start and c == 0,
-                    stop=stop and c == PASSES - 1,
+        q_pool = ctx.enter_context(tc.tile_pool(name="q_pool", bufs=3))
+        soft = ctx.enter_context(tc.tile_pool(name="soft", bufs=3))
+
+        def transpose_k_head(g):
+            k_ps = psum.tile([P, CHUNKS, CHUNK], F32, tag="acc")
+            for ch in range(CHUNKS):
+                nc.tensor.transpose(
+                    k_ps[:, ch, :], qk_rows[ch][:, HEADS + g].rearrange("p a d -> p (a d)"), identity[:]
+                )
+            pairs = k_ps[:].rearrange("p c (G u) -> p (c G) u", u=GROUP)
+            if g // 2 % 4 == 3:
+                nc.vector.tensor_scalar_add(out=k_t[:, :, g, :], in0=pairs, scalar1=k_bias[:, g : g + 1])
+            else:
+                nc.scalar.activation(
+                    out=k_t[:, :, g, :], in_=pairs, func=ACT.Identity, bias=k_bias[:, g : g + 1], scale=1.0
                 )
 
-        for g in range(HEADS):
-            k_acc = psum.tile([P, PAIRS], F32, tag="acc")
-            project(k_acc[:], HEADS + g, 0, slice(0, PAIRS), True, False)
-            project(k_acc[:], HEADS + g, 1, slice(0, PAIRS), False, True)
-            nc.scalar.activation(
-                out=k_t[:, :, g, :],
-                in_=k_acc[:].rearrange("p (G u) -> p G u", u=GROUP),
-                func=ACT.Identity,
-                bias=k_bias[:, g : g + 1],
-                scale=1.0,
-            )
-
-        def project_q_bank(ch, bank, q_s):
-            a, first_head = bank // (HEADS // BANK_HEADS), BANK_HEADS * (bank % (HEADS // BANK_HEADS))
-            q_acc = psum.tile([P, BANK_HEADS, CHUNK], F32, tag="acc")
+        def transpose_q_bank(ch, bank, q_s):
+            heads = slice(BANK_HEADS * bank, BANK_HEADS * (bank + 1))
+            q_ps = psum.tile([P, BANK_HEADS, CHUNK], F32, tag="acc")
             for j in range(BANK_HEADS):
-                project(q_acc[:, j, :], first_head + j, a, slice(CHUNK * ch, CHUNK * (ch + 1)), True, True)
-            heads = slice(first_head, first_head + BANK_HEADS)
-            nc.vector.scalar_tensor_tensor(
-                out=q_s[:, :, a, heads],
-                in0=q_acc[:].rearrange("p h n -> p n h"),
-                scalar=0.125,
-                in1=q_bias[:, a, heads].unsqueeze(1).to_broadcast([P, CHUNK, BANK_HEADS]),
-                op0=ALU.mult,
-                op1=ALU.add,
-            )
+                nc.tensor.transpose(
+                    q_ps[:, j, :],
+                    qk_rows[ch][:, BANK_HEADS * bank + j].rearrange("p a d -> p (a d)"),
+                    identity[:],
+                )
+            for a in range(2):
+                nc.vector.scalar_tensor_tensor(
+                    out=q_s[:, :, a, heads],
+                    in0=q_ps[:].rearrange("p h n -> p n h"),
+                    scalar=q_scale[:, a : a + 1],
+                    in1=q_bias[:, a, heads].unsqueeze(1).to_broadcast([P, CHUNK, BANK_HEADS]),
+                    op0=ALU.mult,
+                    op1=ALU.add,
+                )
 
-        def score_groups(ch, first, count, q_s, score_acc, scores):
-            for i in range(first, first + count):
+        shape = [P, BANK_GROUPS, HEADS]
+
+        def score_bank(first_group, q_s):
+            score_acc = psum.tile([P, BANK_GROUPS, HEADS * GROUP], F32, name="score_acc")
+            for i in range(BANK_GROUPS):
+                local = (first_group + i) % (CHUNK // GROUP)
                 nc.tensor.matmul(
-                    out=score_acc[:, i % BANK_GROUPS],
-                    lhsT=q_s[:, GROUP * i : GROUP * (i + 1)].rearrange("p u a h -> p (u a h)"),
-                    rhs=k_t[:, CHUNK_GROUPS * ch + i].rearrange("p g u -> p (g u)"),
+                    out=score_acc[:, i],
+                    lhsT=q_s[:, GROUP * local : GROUP * (local + 1)].rearrange("p u a h -> p (u a h)"),
+                    rhs=k_t[:, first_group + i].rearrange("p g u -> p (g u)"),
                     start=True,
                     stop=True,
                 )
-            if (first + count) % BANK_GROUPS == 0:
-                groups = slice(first + count - BANK_GROUPS, first + count)
-                for u in range(GROUP):
-                    quadrant = slice(32 * u, 32 * (u + 1))
-                    nc.scalar.copy(
-                        out=scores[quadrant, groups, :],
-                        in_=score_acc[quadrant].rearrange("p G (g u) -> p G g u", u=GROUP)[:, :, :, u],
-                    )
+            scores = soft.tile(shape, F32, name="scores")
+            for u in range(GROUP):
+                quadrant = slice(32 * u, 32 * (u + 1))
+                nc.scalar.copy(
+                    out=scores[quadrant],
+                    in_=score_acc[quadrant].rearrange("p G (g u) -> p G g u", u=GROUP)[:, :, :, u],
+                )
+            return scores
 
-        def softmax_and_store(ch, scores):
-            shape = [P, CHUNK_GROUPS, HEADS]
-            top = soft.tile([P, CHUNK_GROUPS], F32, name="top")
+        def exponentials(scores):
+            top = soft.tile([P, BANK_GROUPS], F32, name="top")
             nc.vector.tensor_reduce(out=top[:], in_=scores[:], axis=AXIS.X, op=ALU.max)
             shifted = soft.tile(shape, F32, name="shifted")
             nc.vector.tensor_tensor(
@@ -225,31 +239,33 @@ def tile_attention_pa_kernel(tc, x, w_qk, b_qk, out):
             )
             weights = soft.tile(shape, F32, name="weights")
             nc.scalar.activation(out=weights[:], in_=shifted[:], func=ACT.Exp)
-            total = soft.tile([P, CHUNK_GROUPS], F32, name="total")
+            return weights
+
+        def normalise_and_store(first_group, weights):
+            total = soft.tile([P, BANK_GROUPS], F32, name="total")
             nc.vector.tensor_reduce(out=total[:], in_=weights[:], axis=AXIS.X, op=ALU.add)
-            inverse = soft.tile([P, CHUNK_GROUPS], F32, name="inverse")
+            inverse = soft.tile([P, BANK_GROUPS], F32, name="inverse")
             nc.vector.reciprocal(out=inverse[:], in_=total[:])
             result = soft.tile(shape, F32, name="result")
             nc.vector.tensor_tensor(
                 out=result[:], in0=weights[:], in1=inverse[:].unsqueeze(2).to_broadcast(shape), op=ALU.mult
             )
-            nc.sync.dma_start(out=out_rows[:, CHUNK_GROUPS * ch : CHUNK_GROUPS * (ch + 1), :], in_=result[:])
+            nc.sync.dma_start(out=out_rows[:, first_group : first_group + BANK_GROUPS, :], in_=result[:])
 
-        q_banks = 2 * HEADS // BANK_HEADS
-        groups_per_bank = CHUNK_GROUPS // q_banks
-        q_tiles = {}
-        for ch in range(CHUNKS + 1):
-            if ch < CHUNKS:
-                q_tiles[ch] = q_pool.tile([P, CHUNK, 2, HEADS], F32, name="q_s")
-            if ch > 0:
-                scores = soft.tile([P, CHUNK_GROUPS, HEADS], F32, name="scores")
-            for bank in range(q_banks):
-                if ch < CHUNKS:
-                    project_q_bank(ch, bank, q_tiles[ch])
-                if ch > 0:
-                    first = groups_per_bank * bank
-                    if first % BANK_GROUPS == 0:
-                        score_acc = psum.tile([P, BANK_GROUPS, HEADS * GROUP], F32, name="score_acc")
-                    score_groups(ch - 1, first, groups_per_bank, q_tiles[ch - 1], score_acc, scores)
-            if ch > 0:
-                softmax_and_store(ch - 1, scores)
+        steps = CHUNKS * Q_BANKS
+        q_tiles, score_tiles, weight_tiles = {}, {}, {}
+        for step in range(steps + LAG + 2):
+            if step < steps:
+                ch, bank = divmod(step, Q_BANKS)
+                if bank == 0:
+                    q_tiles[ch] = q_pool.tile([P, CHUNK, 2, HEADS], F32, name="q_s")
+                transpose_q_bank(ch, bank, q_tiles[ch])
+            if step < LAG:
+                for g in range(HEADS // LAG * step, HEADS // LAG * (step + 1)):
+                    transpose_k_head(g)
+            if 0 <= step - LAG - 2 < steps:
+                normalise_and_store(BANK_GROUPS * (step - LAG - 2), weight_tiles[step - LAG - 2])
+            if 0 <= step - LAG - 1 < steps:
+                weight_tiles[step - LAG - 1] = exponentials(score_tiles[step - LAG - 1])
+            if 0 <= step - LAG < steps:
+                score_tiles[step - LAG] = score_bank(BANK_GROUPS * (step - LAG), q_tiles[(step - LAG) // Q_BANKS])

@@ -82,17 +82,14 @@ def tile_attention_pa_kernel(tc, x, w_qk, b_qk, out):
                 nc.sync.dma_start(out=x_raw[:], in_=rows.rearrange("(r p) c -> p r c", p=P))
                 return x_raw
 
-            def load_w_block(block):
+            def load_w_pass(block, c, w_raw):
                 cols = slice(block * W_BLOCK, (block + 1) * W_BLOCK)
-                w_raw = stage.tile([P, PASSES, 4, W_BLOCK], BF16, name="w_raw")
-                for c in range(PASSES):
-                    for u in range(2):
-                        first = K_PASS * c + 256 * u
-                        nc.sync.dma_start(
-                            out=w_raw[:, c, 2 * u : 2 * u + 2, :],
-                            in_=w_qk[first : first + 256, cols].rearrange("(p e) f -> p e f", e=2),
-                        )
-                return w_raw
+                for u in range(2):
+                    first = K_PASS * c + 256 * u
+                    nc.sync.dma_start(
+                        out=w_raw[:, c, 2 * u : 2 * u + 2, :],
+                        in_=w_qk[first : first + 256, cols].rearrange("(p e) f -> p e f", e=2),
+                    )
 
             def transpose_x_chunk(x_raw):
                 x_grouped = stage.tile([P, PASSES, 2, CHUNK, 4], BF16, name="x_grouped", align_bytes=64)
@@ -118,8 +115,7 @@ def tile_attention_pa_kernel(tc, x, w_qk, b_qk, out):
                     in_=x_grouped[:].rearrange("p c a n t -> p (c a n t)"),
                 )
 
-            def quantise_w_block(block, w_raw):
-                cols = slice(block * W_BLOCK, (block + 1) * W_BLOCK)
+            def group_w_block(w_raw):
                 grouped = []
                 for c in range(PASSES):
                     w_grouped = stage.tile([P, W_BLOCK, 4], BF16, name="w_grouped", align_bytes=64)
@@ -128,6 +124,10 @@ def tile_attention_pa_kernel(tc, x, w_qk, b_qk, out):
                         in_=w_raw[:, c].rearrange("p t (f i) -> p f t i", i=4),
                     )
                     grouped.append(w_grouped)
+                return grouped
+
+            def quantise_w_block(block, grouped):
+                cols = slice(block * W_BLOCK, (block + 1) * W_BLOCK)
                 for c in range(PASSES):
                     nc.vector.quantize_mx(
                         out=w_codes[:, c, cols].bitcast(FP8X4),
@@ -151,25 +151,31 @@ def tile_attention_pa_kernel(tc, x, w_qk, b_qk, out):
                                 start=(c == 0),
                                 stop=(c == PASSES - 1),
                             )
-                        copy_out = nc.vector.tensor_copy if ch == CHUNKS - 1 else nc.scalar.copy
-                        copy_out(out=qk_rows[ch][:, heads, a, :], in_=acc[:])
+                        nc.scalar.copy(out=qk_rows[ch][:, heads, a, :], in_=acc[:])
 
             blocks = (2, 3, 0, 1)
+            w_raws = {}
+            for block in blocks:
+                w_raw = stage.tile([P, PASSES, 4, W_BLOCK], BF16, name="w_raw")
+                w_raws[block] = w_raw
+            load_w_pass(blocks[0], 0, w_raws[blocks[0]])
             x_raws = [load_x_chunk(0)]
-            w_raws = {blocks[0]: load_w_block(blocks[0])}
+            load_w_pass(blocks[0], 1, w_raws[blocks[0]])
             x_raws.extend([load_x_chunk(ch) for ch in range(1, CHUNKS)])
             for block in blocks[1:]:
-                w_raws[block] = load_w_block(block)
+                for c in range(PASSES):
+                    load_w_pass(block, c, w_raws[block])
 
+            grouped = group_w_block(w_raws[blocks[0]])
             x_groupeds = [transpose_x_chunk(x_raws[0])]
             quantise_x_chunk(0, x_groupeds[0])
             x_groupeds.extend([transpose_x_chunk(x_raws[ch]) for ch in range(1, CHUNKS)])
-            quantise_w_block(blocks[0], w_raws[blocks[0]])
+            quantise_w_block(blocks[0], grouped)
             for ch in range(1, CHUNKS):
                 quantise_x_chunk(ch, x_groupeds[ch])
             for i in range(len(blocks)):
                 if i + 1 < len(blocks):
-                    quantise_w_block(blocks[i + 1], w_raws[blocks[i + 1]])
+                    quantise_w_block(blocks[i + 1], group_w_block(w_raws[blocks[i + 1]]))
                 project_block(blocks[i])
 
         q_pool = ctx.enter_context(tc.tile_pool(name="q_pool", bufs=3))
@@ -263,9 +269,11 @@ def tile_attention_pa_kernel(tc, x, w_qk, b_qk, out):
             if step < LAG:
                 for g in range(HEADS // LAG * step, HEADS // LAG * (step + 1)):
                     transpose_k_head(g)
+            if step - LAG - 1 == steps - 1:
+                weight_tiles[step - LAG - 1] = exponentials(score_tiles[step - LAG - 1])
             if 0 <= step - LAG - 2 < steps:
                 normalise_and_store(BANK_GROUPS * (step - LAG - 2), weight_tiles[step - LAG - 2])
-            if 0 <= step - LAG - 1 < steps:
+            if 0 <= step - LAG - 1 < steps - 1:
                 weight_tiles[step - LAG - 1] = exponentials(score_tiles[step - LAG - 1])
             if 0 <= step - LAG < steps:
                 score_tiles[step - LAG] = score_bank(BANK_GROUPS * (step - LAG), q_tiles[(step - LAG) // Q_BANKS])

from contextlib import ExitStack

import concourse.mybir as mybir
from concourse.masks import make_identity

F32 = mybir.dt.float32
BF16 = mybir.dt.bfloat16
U32 = mybir.dt.uint32
U8 = mybir.dt.uint8
FP8X4 = mybir.dt.float8_e4m3fn_x4
ALU = mybir.AluOpType
ACT = mybir.ActivationFunctionType
AXIS = mybir.AxisListType

P = 128
TOKENS = 1024
C = 1024
HEADS = 16
HD = 64
K_PASS = 512
PASSES = C // K_PASS
PAIRS = TOKENS // 2
CHUNK = 128
CHUNKS = PAIRS // CHUNK
W_BLOCK = 512
BLOCK_HEADS = W_BLOCK // HD
GROUP = 4
BANK_GROUPS = 8
BANK_HEADS = 4
Q_BANKS = HEADS // BANK_HEADS
LAG = Q_BANKS

FLOPS = 2 * TOKENS * C * 2 * HEADS * HD + 2 * TOKENS * HEADS * HEADS * HD


def tile_attention_pa_kernel(tc, x, w_qk, b_qk, out):
    nc = tc.nc
    x_rows = x.rearrange("n t c -> (n t) c")
    out_rows = out.rearrange("n t h g -> (n t h) g").rearrange("(G p) g -> p G g", p=P)

    with ExitStack() as ctx:
        ctx.enter_context(tc.manual_schedule())
        keep = ctx.enter_context(tc.tile_pool(name="keep", bufs=1))
        psum = ctx.enter_context(tc.psum_pool(name="psum", bufs=4))

        x_codes = keep.tile([P, CHUNKS, PASSES, 2, CHUNK], U32, align_bytes=64)
        x_scales = keep.tile([P, CHUNKS, PASSES, 2, CHUNK], U8, align_bytes=64)
        w_codes = keep.tile([P, PASSES, 2 * HEADS * HD], U32, align_bytes=64)
        w_scales = keep.tile([P, PASSES, 2 * HEADS * HD], U8, align_bytes=64)
        qk_rows = [keep.tile([P, 2 * HEADS, 2, HD], F32, name="qk_rows%d" % ch) for ch in range(CHUNKS)]
        k_t = keep.tile([P, PAIRS // GROUP, HEADS, GROUP], F32)
        bias_rows = keep.tile([P, P], BF16)
        bias_rows_f32 = keep.tile([P, P], F32)
        k_bias = keep.tile([P, HEADS], F32)
        q_bias = keep.tile([P, 2, HEADS], F32)
        q_scale = keep.tile([P, 2], F32)
        identity = keep.tile([P, P], F32)

        nc.vector.memset(bias_rows[:], 0.0)
        for a in range(2):
            nc.scalar.dma_start(
                out=bias_rows[0 : 2 * HEADS, HD * a : HD * (a + 1)],
                in_=b_qk.rearrange("(f d) -> f d", d=HD),
            )
        make_identity(nc, identity[:])
        nc.vector.memset(q_bias[:], 0.0)
        nc.vector.memset(q_scale[:], 0.0)
        nc.vector.tensor_copy(out=bias_rows_f32[:], in_=bias_rows[:])
        bias_t = psum.tile([P, P], F32, tag="acc")
        nc.tensor.transpose(bias_t[:], bias_rows_f32[:], identity[:])
        nc.vector.tensor_copy(out=k_bias[:], in_=bias_t[:, HEADS : 2 * HEADS])
        for a in range(2):
            half = slice(HD * a, HD * (a + 1))
            nc.vector.memset(q_scale[half, a : a + 1], 0.125)
            nc.vector.tensor_scalar_mul(out=q_bias[half, a, :], in0=bias_t[half, 0:HEADS], scalar1=0.125)

        with tc.tile_pool(name="stage", bufs=4) as stage:

            def load_x_chunk(ch):
                x_raw = stage.tile([P, 2, C], BF16, name="x_raw")
                rows = x_rows[2 * CHUNK * ch : 2 * CHUNK * (ch + 1), :]
                nc.sync.dma_start(out=x_raw[:], in_=rows.rearrange("(r p) c -> p r c", p=P))
                return x_raw

            def load_w_pass(block, c, w_raw):
                cols = slice(block * W_BLOCK, (block + 1) * W_BLOCK)
                for u in range(2):
                    first = K_PASS * c + 256 * u
                    nc.sync.dma_start(
                        out=w_raw[:, c, 2 * u : 2 * u + 2, :],
                        in_=w_qk[first : first + 256, cols].rearrange("(p e) f -> p e f", e=2),
                    )

            def transpose_x_chunk(x_raw):
                x_grouped = stage.tile([P, PASSES, 2, CHUNK, 4], BF16, name="x_grouped", align_bytes=64)
                x_grouped_words = x_grouped[:].bitcast(F32)
                for r in range(2):
                    words = x_raw[:, r, :].bitcast(F32)
                    x_t = psum.tile([P, PASSES, 2, P], F32, tag="acc")
                    for c in range(PASSES):
                        for u in range(2):
                            first = 256 * c + P * u
                            nc.tensor.transpose(x_t[:, c, u, :], words[:, first : first + P], identity[:])
                    for c in range(PASSES):
                        nc.scalar.copy(
                            out=x_grouped_words[:, c, :, 64 * r : 64 * (r + 1), :],
                            in_=x_t[:, c].rearrange("p u (m a) -> p a m u", a=2),
                        )
                return x_grouped

            def quantise_x_chunk(ch, x_grouped):
                nc.vector.quantize_mx(
                    out=x_codes[:, ch].rearrange("p c a n -> p (c a n)").bitcast(FP8X4),
                    scales=x_scales[:, ch].rearrange("p c a n -> p (c a n)"),
                    in_=x_grouped[:].rearrange("p c a n t -> p (c a n t)"),
                )

            def group_w_block(w_raw):
                grouped = []
                for c in range(PASSES):
                    w_grouped = stage.tile([P, W_BLOCK, 4], BF16, name="w_grouped", align_bytes=64)
                    nc.vector.tensor_copy(
                        out=w_grouped[:].rearrange("p (f i) t -> p f t i", i=4),
                        in_=w_raw[:, c].rearrange("p t (f i) -> p f t i", i=4),
                    )
                    grouped.append(w_grouped)
                return grouped

            def quantise_w_block(block, grouped):
                cols = slice(block * W_BLOCK, (block + 1) * W_BLOCK)
                for c in range(PASSES):
                    nc.vector.quantize_mx(
                        out=w_codes[:, c, cols].bitcast(FP8X4),
                        scales=w_scales[:, c, cols],
                        in_=grouped[c][:].rearrange("p f t -> p (f t)"),
                    )

            def project_block(block):
                cols = slice(block * W_BLOCK, (block + 1) * W_BLOCK)
                heads = slice(block * BLOCK_HEADS, (block + 1) * BLOCK_HEADS)
                for ch in range(CHUNKS):
                    for a in range(2):
                        acc = psum.tile([P, BLOCK_HEADS, HD], F32, tag="acc")
                        for c in range(PASSES):
                            nc.tensor.matmul_mx(
                                out=acc[:].rearrange("p h d -> p (h d)"),
                                lhsT=x_codes[:, ch, c, a, :].bitcast(FP8X4),
                                lhsT_scale=x_scales[:, ch, c, a, :],
                                rhs=w_codes[:, c, cols].bitcast(FP8X4),
                                rhs_scale=w_scales[:, c, cols],
                                start=(c == 0),
                                stop=(c == PASSES - 1),
                            )
                        nc.scalar.copy(out=qk_rows[ch][:, heads, a, :], in_=acc[:])

            blocks = (2, 3, 0, 1)
            w_raws = {}
            for block in blocks:
                w_raw = stage.tile([P, PASSES, 4, W_BLOCK], BF16, name="w_raw")
                w_raws[block] = w_raw
            load_w_pass(blocks[0], 0, w_raws[blocks[0]])
            x_raws = [load_x_chunk(0)]
            load_w_pass(blocks[0], 1, w_raws[blocks[0]])
            x_raws.extend([load_x_chunk(ch) for ch in range(1, CHUNKS)])
            for block in blocks[1:]:
                for c in range(PASSES):
                    load_w_pass(block, c, w_raws[block])

            grouped = group_w_block(w_raws[blocks[0]])
            x_groupeds = [transpose_x_chunk(x_raws[0])]
            quantise_x_chunk(0, x_groupeds[0])
            x_groupeds.extend([transpose_x_chunk(x_raws[ch]) for ch in range(1, CHUNKS)])
            quantise_w_block(blocks[0], grouped)
            for ch in range(1, CHUNKS):
                quantise_x_chunk(ch, x_groupeds[ch])
            for i in range(len(blocks)):
                if i + 1 < len(blocks):
                    quantise_w_block(blocks[i + 1], group_w_block(w_raws[blocks[i + 1]]))
                project_block(blocks[i])

        q_pool = ctx.enter_context(tc.tile_pool(name="q_pool", bufs=3))
        soft = ctx.enter_context(tc.tile_pool(name="soft", bufs=3))

        def transpose_k_head(g):
            k_ps = psum.tile([P, CHUNKS, CHUNK], F32, tag="acc")
            for ch in range(CHUNKS):
                nc.tensor.transpose(
                    k_ps[:, ch, :], qk_rows[ch][:, HEADS + g].rearrange("p a d -> p (a d)"), identity[:]
                )
            pairs = k_ps[:].rearrange("p c (G u) -> p (c G) u", u=GROUP)
            if g // 2 % 4 == 3:
                nc.vector.tensor_scalar_add(out=k_t[:, :, g, :], in0=pairs, scalar1=k_bias[:, g : g + 1])
            else:
                nc.scalar.activation(
                    out=k_t[:, :, g, :], in_=pairs, func=ACT.Identity, bias=k_bias[:, g : g + 1], scale=1.0
                )

        def transpose_q_bank(ch, bank, q_s):
            heads = slice(BANK_HEADS * bank, BANK_HEADS * (bank + 1))
            q_ps = psum.tile([P, BANK_HEADS, CHUNK], F32, tag="acc")
            for j in range(BANK_HEADS):
                nc.tensor.transpose(
                    q_ps[:, j, :],
                    qk_rows[ch][:, BANK_HEADS * bank + j].rearrange("p a d -> p (a d)"),
                    identity[:],
                )
            for a in range(2):
                nc.vector.scalar_tensor_tensor(
                    out=q_s[:, :, a, heads],
                    in0=q_ps[:].rearrange("p h n -> p n h"),
                    scalar=q_scale[:, a : a + 1],
                    in1=q_bias[:, a, heads].unsqueeze(1).to_broadcast([P, CHUNK, BANK_HEADS]),
                    op0=ALU.mult,
                    op1=ALU.add,
                )

        shape = [P, BANK_GROUPS, HEADS]

        def score_bank(first_group, q_s):
            score_acc = psum.tile([P, BANK_GROUPS, HEADS * GROUP], F32, name="score_acc")
            for i in range(BANK_GROUPS):
                local = (first_group + i) % (CHUNK // GROUP)
                nc.tensor.matmul(
                    out=score_acc[:, i],
                    lhsT=q_s[:, GROUP * local : GROUP * (local + 1)].rearrange("p u a h -> p (u a h)"),
                    rhs=k_t[:, first_group + i].rearrange("p g u -> p (g u)"),
                    start=True,
                    stop=True,
                )
            scores = soft.tile(shape, F32, name="scores")
            for u in range(GROUP):
                quadrant = slice(32 * u, 32 * (u + 1))
                nc.scalar.copy(
                    out=scores[quadrant],
                    in_=score_acc[quadrant].rearrange("p G (g u) -> p G g u", u=GROUP)[:, :, :, u],
                )
            return scores

        def exponentials(scores):
            top = soft.tile([P, BANK_GROUPS], F32, name="top")
            nc.vector.tensor_reduce(out=top[:], in_=scores[:], axis=AXIS.X, op=ALU.max)
            shifted = soft.tile(shape, F32, name="shifted")
            nc.vector.tensor_tensor(
                out=shifted[:], in0=scores[:], in1=top[:].unsqueeze(2).to_broadcast(shape), op=ALU.subtract
            )
            weights = soft.tile(shape, F32, name="weights")
            nc.scalar.activation(out=weights[:], in_=shifted[:], func=ACT.Exp)
            return weights

        def normalise_and_store(first_group, weights):
            total = soft.tile([P, BANK_GROUPS], F32, name="total")
            nc.vector.tensor_reduce(out=total[:], in_=weights[:], axis=AXIS.X, op=ALU.add)
            inverse = soft.tile([P, BANK_GROUPS], F32, name="inverse")
            nc.vector.reciprocal(out=inverse[:], in_=total[:])
            result = soft.tile(shape, F32, name="result")
            nc.vector.tensor_tensor(
                out=result[:], in0=weights[:], in1=inverse[:].unsqueeze(2).to_broadcast(shape), op=ALU.mult
            )
            nc.sync.dma_start(out=out_rows[:, first_group : first_group + BANK_GROUPS, :], in_=result[:])

        steps = CHUNKS * Q_BANKS
        q_tiles, score_tiles, weight_tiles = {}, {}, {}
        for step in range(steps + LAG + 2):
            if step < steps:
                ch, bank = divmod(step, Q_BANKS)
                if bank == 0:
                    q_tiles[ch] = q_pool.tile([P, CHUNK, 2, HEADS], F32, name="q_s")
                transpose_q_bank(ch, bank, q_tiles[ch])
            if step < LAG:
                for g in range(HEADS // LAG * step, HEADS // LAG * (step + 1)):
                    transpose_k_head(g)
            if step - LAG - 1 == steps - 1:
                weight_tiles[step - LAG - 1] = exponentials(score_tiles[step - LAG - 1])
            if 0 <= step - LAG - 2 < steps:
                normalise_and_store(BANK_GROUPS * (step - LAG - 2), weight_tiles[step - LAG - 2])
            if 0 <= step - LAG - 1 < steps - 1:
                weight_tiles[step - LAG - 1] = exponentials(score_tiles[step - LAG - 1])
            if 0 <= step - LAG < steps:
                score_tiles[step - LAG] = score_bank(BANK_GROUPS * (step - LAG), q_tiles[(step - LAG) // Q_BANKS])
